import numpy as np
import ml_dtypes


def mxq(x, axis, fmt="e4m3"):
    dtype, down = {"e4m3": (ml_dtypes.float8_e4m3fn, 7), "e5m2": (ml_dtypes.float8_e5m2, 14)}[fmt]
    v = np.moveaxis(np.asarray(x, np.float32).astype(ml_dtypes.bfloat16).astype(np.float64), axis, -1)
    blocks = v.reshape(v.shape[:-1] + (-1, 32))
    amax = np.abs(blocks).max(-1, keepdims=True)
    byte = np.maximum(np.where(amax > 0, np.frexp(amax)[1] - 1 + 127, 0) - down, 1)
    scale = np.exp2(byte - 127.0)
    codes = (blocks / scale).astype(np.float32).astype(dtype).astype(np.float64)
    return np.moveaxis((codes * scale).reshape(v.shape), -1, axis)


WIDE = False


def mx_kscale(k):
    if not WIDE:
        return np.ones(k)
    levels = np.array([10, -10, 5, -5, 0])
    a = np.random.permutation(np.resize(levels, k // 512 * 4)).reshape(k // 512, 4)
    idx = np.arange(k)
    return np.exp2(a[idx // 512, idx % 128 // 32])


BF16 = ml_dtypes.bfloat16


def bf(x):
    return np.asarray(x, np.float32).astype(BF16)


def f64(x):
    return np.asarray(x).astype(np.float64)


N, P, D, E, F = 1024, 3, 512, 1024, 1024


def setup_inputs():
    s = mx_kscale(D)
    x = np.random.standard_normal((N, P, D)) + 0.5 * np.random.standard_normal((1, P, D))
    return {"x": bf(x * s),
            "w1a": bf(np.random.standard_normal((D, E)) / np.sqrt(D) / s[:, None]),
            "w2a": bf(np.random.standard_normal((D, E)) / np.sqrt(D) / s[:, None])}


def reference(x, w1a, w2a):
    h = f64(x)
    neigh = (h.sum(axis=1, keepdims=True) - h) * 0.5
    return (mxq(h, 2, "e4m3") @ mxq(f64(w2a), 0, "e4m3")) + (mxq(neigh, 2, "e4m3") @ mxq(f64(w1a), 0, "e4m3"))

@@ -1,0 +1,189 @@
+from contextlib import ExitStack
+
+import concourse.mybir as mybir
+from concourse.masks import make_identity
+
+F32 = mybir.dt.float32
+BF16 = mybir.dt.bfloat16
+U32 = mybir.dt.uint32
+U8 = mybir.dt.uint8
+FP8X4 = mybir.dt.float8_e4m3fn_x4
+ADD = mybir.AluOpType.add
+MULT = mybir.AluOpType.mult
+
+P = 128
+PACK = 4
+ITEMS, HOPS, K, E = 1024, 3, 512, 1024
+WORDS = K // 2
+TILES = ITEMS // P
+N_PASS = 512
+HALVES = E // N_PASS
+W_CHUNK = 256
+RUN = 4
+LEAD = 2
+
+FLOPS = 2 * 2 * ITEMS * HOPS * K * E
+
+
+def load_weight(nc, raw, w):
+    nc.sync.dma_start(
+        out=raw[:].rearrange("q (u e) c -> q u e c", u=2),
+        in_=w.rearrange("(u q e) c -> q u e c", u=2, e=2),
+    )
+
+
+def quantise_weight(nc, raw, grouped, codes, scales):
+    chunks = [slice(j * W_CHUNK, (j + 1) * W_CHUNK) for j in range(E // W_CHUNK)]
+    for j, cols in enumerate(chunks):
+        copy = nc.vector.tensor_copy if j % 2 == 0 else nc.scalar.copy
+        copy(
+            out=grouped[:, cols, :].rearrange("q (c i) t -> q c t i", i=RUN),
+            in_=raw[:, :, cols].rearrange("q t (c i) -> q c t i", i=RUN),
+        )
+    for cols in chunks:
+        nc.vector.quantize_mx(
+            out=codes[:, cols].bitcast(FP8X4),
+            scales=scales[:, cols],
+            in_=grouped[:, cols, :].rearrange("q c t -> q (c t)"),
+        )
+
+
+def tile_dogtaitujuanji_pa_kernel(tc, x, w1a, w2a, out):
+    nc = tc.nc
+    with ExitStack() as ctx:
+        keep = ctx.enter_context(tc.tile_pool(name="keep", bufs=1))
+        rows = ctx.enter_context(tc.tile_pool(name="rows", bufs=TILES))
+        work = ctx.enter_context(tc.tile_pool(name="work", bufs=2))
+        operands = ctx.enter_context(tc.tile_pool(name="operands", bufs=LEAD + 2))
+        results = ctx.enter_context(tc.tile_pool(name="results", bufs=6))
+        flipped = ctx.enter_context(tc.psum_pool(name="flipped", bufs=HOPS))
+        sums = ctx.enter_context(tc.psum_pool(name="sums", bufs=8 - HOPS))
+
+        w2a_raw = keep.tile([P, PACK, E], BF16)
+        w1a_raw = keep.tile([P, PACK, E], BF16)
+        x_rows = []
+        for i in range(TILES):
+            x_tile = rows.tile([P, HOPS * K], BF16, name="x_tile")
+            x_rows.append(x_tile)
+
+        def load_x(i):
+            nc.sync.dma_start(
+                out=x_rows[i][:], in_=x[i * P : (i + 1) * P].rearrange("n p k -> n (p k)")
+            )
+
+        load_weight(nc, w2a_raw, w2a)
+        load_x(0)
+        load_weight(nc, w1a_raw, w1a)
+        for i in range(1, TILES):
+            load_x(i)
+
+        identity = keep.tile([P, P], F32)
+        make_identity(nc, identity[:])
+
+        w2a_grouped = keep.tile([P, E, PACK], BF16, align_bytes=64)
+        w1a_grouped = keep.tile([P, E, PACK], BF16, align_bytes=64)
+        w2a_codes = keep.tile([P, E], U32, align_bytes=64)
+        w1a_codes = keep.tile([P, E], U32, align_bytes=64)
+        w2a_scales = keep.tile([P, E], U8, align_bytes=64)
+        w1a_scales = keep.tile([P, E], U8, align_bytes=64)
+
+        prepared = {}
+
+        def prepare(i, copy_out):
+            x_words = x_rows[i][:].bitcast(F32)
+            x_t = work.tile([P, HOPS * P * PACK], BF16, align_bytes=64)
+            x_t_words = x_t[:].bitcast(F32)
+            banks = []
+            for p in range(HOPS):
+                bank = flipped.tile([P, 2, P], F32, name="bank")
+                for u in range(2):
+                    first = p * WORDS + u * P
+                    nc.tensor.transpose(bank[:, u, :], x_words[:, first : first + P], identity[:])
+                banks.append(bank)
+            for p in range(HOPS):
+                copy_out(
+                    out=x_t_words[:, p * 2 * P : (p + 1) * 2 * P].rearrange(
+                        "q (n u) -> q n u", u=2
+                    ),
+                    in_=banks[p][:].rearrange("q u n -> q n u"),
+                )
+
+            x_codes = operands.tile([P, HOPS * P], U32, align_bytes=64)
+            x_scales = operands.tile([P, HOPS * P], U8, align_bytes=64)
+            n_codes = operands.tile([P, HOPS * P], U32, align_bytes=64)
+            n_scales = operands.tile([P, HOPS * P], U8, align_bytes=64)
+            width = P * PACK
+
+            half = work.tile([P, HOPS, width], BF16)
+            nc.vector.tensor_scalar(
+                out=half[:].rearrange("q p w -> q (p w)"),
+                in0=x_t[:],
+                scalar1=0.5,
+                scalar2=None,
+                op0=MULT,
+            )
+            for p in range(HOPS):
+                nc.vector.quantize_mx(
+                    out=x_codes[:, p * P : (p + 1) * P].bitcast(FP8X4),
+                    scales=x_scales[:, p * P : (p + 1) * P],
+                    in_=x_t[:, p * width : (p + 1) * width],
+                )
+            neigh = work.tile([P, HOPS, width], BF16, align_bytes=64)
+            nc.vector.tensor_tensor(
+                out=neigh[:, 0:2, :], in0=half[:, 0:2, :], in1=half[:, 1:3, :], op=ADD
+            )
+            nc.vector.tensor_tensor(
+                out=neigh[:, 2, :], in0=half[:, 2, :], in1=half[:, 0, :], op=ADD
+            )
+            for s in range(HOPS):
+                nc.vector.quantize_mx(
+                    out=n_codes[:, s * P : (s + 1) * P].bitcast(FP8X4),
+                    scales=n_scales[:, s * P : (s + 1) * P],
+                    in_=neigh[:, s, :],
+                )
+            prepared[i] = (x_codes, x_scales, n_codes, n_scales)
+
+        def multiply(i):
+            x_codes, x_scales, n_codes, n_scales = prepared[i]
+            vector_is_free = i + LEAD >= TILES
+            for p in range(HOPS):
+                own = slice(p * P, (p + 1) * P)
+                slot = (p + 1) % HOPS
+                others = slice(slot * P, (slot + 1) * P)
+                result = results.tile([P, E], F32)
+                for c in range(HALVES):
+                    cols = slice(c * N_PASS, (c + 1) * N_PASS)
+                    acc = sums.tile([P, N_PASS], F32)
+                    nc.tensor.matmul_mx(
+                        out=acc[:],
+                        lhsT=x_codes[:, own].bitcast(FP8X4),
+                        lhsT_scale=x_scales[:, own],
+                        rhs=w2a_codes[:, cols].bitcast(FP8X4),
+                        rhs_scale=w2a_scales[:, cols],
+                        start=True,
+                        stop=False,
+                    )
+                    nc.tensor.matmul_mx(
+                        out=acc[:],
+                        lhsT=n_codes[:, others].bitcast(FP8X4),
+                        lhsT_scale=n_scales[:, others],
+                        rhs=w1a_codes[:, cols].bitcast(FP8X4),
+                        rhs_scale=w1a_scales[:, cols],
+                        start=False,
+                        stop=True,
+                    )
+                    if vector_is_free and c == 1:
+                        nc.vector.tensor_copy(out=result[:, cols], in_=acc[:])
+                    else:
+                        nc.scalar.copy(out=result[:, cols], in_=acc[:])
+                nc.sync.dma_start(out=out[i * P : (i + 1) * P, p, :], in_=result[:])
+
+        quantise_weight(nc, w2a_raw, w2a_grouped, w2a_codes, w2a_scales)
+        prepare(0, nc.scalar.copy)
+        quantise_weight(nc, w1a_raw, w1a_grouped, w1a_codes, w1a_scales)
+        for i in range(1, LEAD):
+            prepare(i, nc.scalar.copy)
+        for i in range(TILES):
+            if i + LEAD < TILES:
+                prepare(i + LEAD, nc.vector.tensor_copy)
+            multiply(i)

@@ -58,6 +58,7 @@ def tile_dogtaitujuanji_pa_kernel(tc, x, w1a, w2a, out):
         results = ctx.enter_context(tc.tile_pool(name="results", bufs=6))
         flipped = ctx.enter_context(tc.psum_pool(name="flipped", bufs=HOPS))
         sums = ctx.enter_context(tc.psum_pool(name="sums", bufs=8 - HOPS))
+        ctx.enter_context(tc.manual_schedule())
 
         w2a_raw = keep.tile([P, PACK, E], BF16)
         w1a_raw = keep.tile([P, PACK, E], BF16)

@@ -20,7 +20,7 @@ N_PASS = 512
 HALVES = E // N_PASS
 W_CHUNK = 256
 RUN = 4
-LEAD = 2
+AHEAD = 2
 
 FLOPS = 2 * 2 * ITEMS * HOPS * K * E
 
@@ -32,20 +32,22 @@ def load_weight(nc, raw, w):
     )
 
 
-def quantise_weight(nc, raw, grouped, codes, scales):
-    chunks = [slice(j * W_CHUNK, (j + 1) * W_CHUNK) for j in range(E // W_CHUNK)]
-    for j, cols in enumerate(chunks):
-        copy = nc.vector.tensor_copy if j % 2 == 0 else nc.scalar.copy
+def regroup_weight(nc, raw, grouped, c):
+    for copy, first in ((nc.vector.tensor_copy, c * N_PASS), (nc.scalar.copy, c * N_PASS + W_CHUNK)):
+        cols = slice(first, first + W_CHUNK)
         copy(
             out=grouped[:, cols, :].rearrange("q (c i) t -> q c t i", i=RUN),
             in_=raw[:, :, cols].rearrange("q t (c i) -> q c t i", i=RUN),
         )
-    for cols in chunks:
-        nc.vector.quantize_mx(
-            out=codes[:, cols].bitcast(FP8X4),
-            scales=scales[:, cols],
-            in_=grouped[:, cols, :].rearrange("q c t -> q (c t)"),
-        )
+
+
+def quantise_weight(nc, grouped, codes, scales, c):
+    cols = slice(c * N_PASS, (c + 1) * N_PASS)
+    nc.vector.quantize_mx(
+        out=codes[:, cols].bitcast(FP8X4),
+        scales=scales[:, cols],
+        in_=grouped[:, cols, :].rearrange("q c t -> q (c t)"),
+    )
 
 
 def tile_dogtaitujuanji_pa_kernel(tc, x, w1a, w2a, out):
@@ -53,8 +55,9 @@ def tile_dogtaitujuanji_pa_kernel(tc, x, w1a, w2a, out):
     with ExitStack() as ctx:
         keep = ctx.enter_context(tc.tile_pool(name="keep", bufs=1))
         rows = ctx.enter_context(tc.tile_pool(name="rows", bufs=TILES))
+        turns = ctx.enter_context(tc.tile_pool(name="turns", bufs=AHEAD + 1))
         work = ctx.enter_context(tc.tile_pool(name="work", bufs=2))
-        operands = ctx.enter_context(tc.tile_pool(name="operands", bufs=LEAD + 2))
+        operands = ctx.enter_context(tc.tile_pool(name="operands", bufs=AHEAD + 2))
         results = ctx.enter_context(tc.tile_pool(name="results", bufs=6))
         flipped = ctx.enter_context(tc.psum_pool(name="flipped", bufs=HOPS))
         sums = ctx.enter_context(tc.psum_pool(name="sums", bufs=8 - HOPS))
@@ -67,16 +70,21 @@ def tile_dogtaitujuanji_pa_kernel(tc, x, w1a, w2a, out):
             x_tile = rows.tile([P, HOPS * K], BF16, name="x_tile")
             x_rows.append(x_tile)
 
-        def load_x(i):
+        def load_x(i, first_hop, hops):
             nc.sync.dma_start(
-                out=x_rows[i][:], in_=x[i * P : (i + 1) * P].rearrange("n p k -> n (p k)")
+                out=x_rows[i][:, first_hop * K : (first_hop + hops) * K],
+                in_=x[i * P : (i + 1) * P, first_hop : first_hop + hops, :].rearrange(
+                    "n p k -> n (p k)"
+                ),
             )
 
+        for p in range(HOPS):
+            load_x(0, p, 1)
         load_weight(nc, w2a_raw, w2a)
-        load_x(0)
+        load_x(1, 0, HOPS)
         load_weight(nc, w1a_raw, w1a)
-        for i in range(1, TILES):
-            load_x(i)
+        for i in range(2, TILES):
+            load_x(i, 0, HOPS)
 
         identity = keep.tile([P, P], F32)
         make_identity(nc, identity[:])
@@ -88,11 +96,13 @@ def tile_dogtaitujuanji_pa_kernel(tc, x, w1a, w2a, out):
         w2a_scales = keep.tile([P, E], U8, align_bytes=64)
         w1a_scales = keep.tile([P, E], U8, align_bytes=64)
 
+        width = P * PACK
+        turned = {}
         prepared = {}
 
-        def prepare(i, copy_out):
+        def turn(i, copy_out):
             x_words = x_rows[i][:].bitcast(F32)
-            x_t = work.tile([P, HOPS * P * PACK], BF16, align_bytes=64)
+            x_t = turns.tile([P, HOPS * width], BF16, align_bytes=64)
             x_t_words = x_t[:].bitcast(F32)
             banks = []
             for p in range(HOPS):
@@ -108,13 +118,24 @@ def tile_dogtaitujuanji_pa_kernel(tc, x, w1a, w2a, out):
                     ),
                     in_=banks[p][:].rearrange("q u n -> q n u"),
                 )
+            turned[i] = x_t
 
+        def quantise_tile(i):
+            x_t = turned[i]
             x_codes = operands.tile([P, HOPS * P], U32, align_bytes=64)
             x_scales = operands.tile([P, HOPS * P], U8, align_bytes=64)
             n_codes = operands.tile([P, HOPS * P], U32, align_bytes=64)
             n_scales = operands.tile([P, HOPS * P], U8, align_bytes=64)
-            width = P * PACK
 
+            def quantise_x(p):
+                nc.vector.quantize_mx(
+                    out=x_codes[:, p * P : (p + 1) * P].bitcast(FP8X4),
+                    scales=x_scales[:, p * P : (p + 1) * P],
+                    in_=x_t[:, p * width : (p + 1) * width],
+                )
+
+            quantise_x(0)
+            quantise_x(1)
             half = work.tile([P, HOPS, width], BF16)
             nc.vector.tensor_scalar(
                 out=half[:].rearrange("q p w -> q (p w)"),
@@ -123,12 +144,7 @@ def tile_dogtaitujuanji_pa_kernel(tc, x, w1a, w2a, out):
                 scalar2=None,
                 op0=MULT,
             )
-            for p in range(HOPS):
-                nc.vector.quantize_mx(
-                    out=x_codes[:, p * P : (p + 1) * P].bitcast(FP8X4),
-                    scales=x_scales[:, p * P : (p + 1) * P],
-                    in_=x_t[:, p * width : (p + 1) * width],
-                )
+            quantise_x(2)
             neigh = work.tile([P, HOPS, width], BF16, align_bytes=64)
             nc.vector.tensor_tensor(
                 out=neigh[:, 0:2, :], in0=half[:, 0:2, :], in1=half[:, 1:3, :], op=ADD
@@ -144,47 +160,62 @@ def tile_dogtaitujuanji_pa_kernel(tc, x, w1a, w2a, out):
                 )
             prepared[i] = (x_codes, x_scales, n_codes, n_scales)
 
-        def multiply(i):
+        def multiply(i, p):
             x_codes, x_scales, n_codes, n_scales = prepared[i]
-            vector_is_free = i + LEAD >= TILES
-            for p in range(HOPS):
-                own = slice(p * P, (p + 1) * P)
-                slot = (p + 1) % HOPS
-                others = slice(slot * P, (slot + 1) * P)
-                result = results.tile([P, E], F32)
-                for c in range(HALVES):
-                    cols = slice(c * N_PASS, (c + 1) * N_PASS)
-                    acc = sums.tile([P, N_PASS], F32)
-                    nc.tensor.matmul_mx(
-                        out=acc[:],
-                        lhsT=x_codes[:, own].bitcast(FP8X4),
-                        lhsT_scale=x_scales[:, own],
-                        rhs=w2a_codes[:, cols].bitcast(FP8X4),
-                        rhs_scale=w2a_scales[:, cols],
-                        start=True,
-                        stop=False,
-                    )
-                    nc.tensor.matmul_mx(
-                        out=acc[:],
-                        lhsT=n_codes[:, others].bitcast(FP8X4),
-                        lhsT_scale=n_scales[:, others],
-                        rhs=w1a_codes[:, cols].bitcast(FP8X4),
-                        rhs_scale=w1a_scales[:, cols],
-                        start=False,
-                        stop=True,
-                    )
-                    if vector_is_free and c == 1:
-                        nc.vector.tensor_copy(out=result[:, cols], in_=acc[:])
-                    else:
-                        nc.scalar.copy(out=result[:, cols], in_=acc[:])
-                nc.sync.dma_start(out=out[i * P : (i + 1) * P, p, :], in_=result[:])
+            items = slice(i * P, (i + 1) * P)
+            own = slice(p * P, (p + 1) * P)
+            slot = (p + 1) % HOPS
+            others = slice(slot * P, (slot + 1) * P)
+            result = results.tile([P, E], F32)
+            for c in range(HALVES):
+                cols = slice(c * N_PASS, (c + 1) * N_PASS)
+                acc = sums.tile([P, N_PASS], F32)
+                nc.tensor.matmul_mx(
+                    out=acc[:],
+                    lhsT=x_codes[:, own].bitcast(FP8X4),
+                    lhsT_scale=x_scales[:, own],
+                    rhs=w2a_codes[:, cols].bitcast(FP8X4),
+                    rhs_scale=w2a_scales[:, cols],
+                    start=True,
+                    stop=False,
+                )
+                nc.tensor.matmul_mx(
+                    out=acc[:],
+                    lhsT=n_codes[:, others].bitcast(FP8X4),
+                    lhsT_scale=n_scales[:, others],
+                    rhs=w1a_codes[:, cols].bitcast(FP8X4),
+                    rhs_scale=w1a_scales[:, cols],
+                    start=False,
+                    stop=True,
+                )
+                if i + AHEAD >= TILES and c == 1:
+                    nc.vector.tensor_copy(out=result[:, cols], in_=acc[:])
+                else:
+                    nc.scalar.copy(out=result[:, cols], in_=acc[:])
+                if i == TILES - 1:
+                    nc.sync.dma_start(out=out[items, p, cols], in_=result[:, cols])
+            if i < TILES - 1:
+                nc.sync.dma_start(out=out[items, p, :], in_=result[:])
 
-        quantise_weight(nc, w2a_raw, w2a_grouped, w2a_codes, w2a_scales)
-        prepare(0, nc.scalar.copy)
-        quantise_weight(nc, w1a_raw, w1a_grouped, w1a_codes, w1a_scales)
-        for i in range(1, LEAD):
-            prepare(i, nc.scalar.copy)
+        turn(0, nc.scalar.copy)
+        quantise_tile(0)
+        for c in range(HALVES):
+            regroup_weight(nc, w2a_raw, w2a_grouped, c)
+        turn(1, nc.scalar.copy)
+        for c in range(HALVES):
+            quantise_weight(nc, w2a_grouped, w2a_codes, w2a_scales, c)
+        for c in range(HALVES):
+            regroup_weight(nc, w1a_raw, w1a_grouped, c)
+        for c in range(HALVES):
+            quantise_weight(nc, w1a_grouped, w1a_codes, w1a_scales, c)
+        quantise_tile(1)
+        turn(AHEAD, nc.vector.tensor_copy)
+
         for i in range(TILES):
-            if i + LEAD < TILES:
-                prepare(i + LEAD, nc.vector.tensor_copy)
-            multiply(i)
+            multiply(i, 0)
+            if AHEAD < i + AHEAD < TILES:
+                turn(i + AHEAD, nc.vector.tensor_copy)
+            if i + AHEAD < TILES:
+                quantise_tile(i + AHEAD)
+            for p in range(1, HOPS):
+                multiply(i, p)

from contextlib import ExitStack

import concourse.mybir as mybir
from concourse.masks import make_identity

F32 = mybir.dt.float32
BF16 = mybir.dt.bfloat16
U32 = mybir.dt.uint32
U8 = mybir.dt.uint8
FP8X4 = mybir.dt.float8_e4m3fn_x4
ADD = mybir.AluOpType.add
MULT = mybir.AluOpType.mult

P = 128
PACK = 4
ITEMS, HOPS, K, E = 1024, 3, 512, 1024
WORDS = K // 2
TILES = ITEMS // P
N_PASS = 512
HALVES = E // N_PASS
W_CHUNK = 256
RUN = 4
AHEAD = 2

FLOPS = 2 * 2 * ITEMS * HOPS * K * E


def load_weight(nc, raw, w):
    nc.sync.dma_start(
        out=raw[:].rearrange("q (u e) c -> q u e c", u=2),
        in_=w.rearrange("(u q e) c -> q u e c", u=2, e=2),
    )


def regroup_weight(nc, raw, grouped, c):
    for copy, first in ((nc.vector.tensor_copy, c * N_PASS), (nc.scalar.copy, c * N_PASS + W_CHUNK)):
        cols = slice(first, first + W_CHUNK)
        copy(
            out=grouped[:, cols, :].rearrange("q (c i) t -> q c t i", i=RUN),
            in_=raw[:, :, cols].rearrange("q t (c i) -> q c t i", i=RUN),
        )


def quantise_weight(nc, grouped, codes, scales, c):
    cols = slice(c * N_PASS, (c + 1) * N_PASS)
    nc.vector.quantize_mx(
        out=codes[:, cols].bitcast(FP8X4),
        scales=scales[:, cols],
        in_=grouped[:, cols, :].rearrange("q c t -> q (c t)"),
    )


def tile_dogtaitujuanji_pa_kernel(tc, x, w1a, w2a, out):
    nc = tc.nc
    with ExitStack() as ctx:
        keep = ctx.enter_context(tc.tile_pool(name="keep", bufs=1))
        rows = ctx.enter_context(tc.tile_pool(name="rows", bufs=TILES))
        turns = ctx.enter_context(tc.tile_pool(name="turns", bufs=AHEAD + 1))
        work = ctx.enter_context(tc.tile_pool(name="work", bufs=2))
        operands = ctx.enter_context(tc.tile_pool(name="operands", bufs=AHEAD + 2))
        results = ctx.enter_context(tc.tile_pool(name="results", bufs=6))
        flipped = ctx.enter_context(tc.psum_pool(name="flipped", bufs=HOPS))
        sums = ctx.enter_context(tc.psum_pool(name="sums", bufs=8 - HOPS))
        ctx.enter_context(tc.manual_schedule())

        w2a_raw = keep.tile([P, PACK, E], BF16)
        w1a_raw = keep.tile([P, PACK, E], BF16)
        x_rows = []
        for i in range(TILES):
            x_tile = rows.tile([P, HOPS * K], BF16, name="x_tile")
            x_rows.append(x_tile)

        def load_x(i, first_hop, hops):
            nc.sync.dma_start(
                out=x_rows[i][:, first_hop * K : (first_hop + hops) * K],
                in_=x[i * P : (i + 1) * P, first_hop : first_hop + hops, :].rearrange(
                    "n p k -> n (p k)"
                ),
            )

        for p in range(HOPS):
            load_x(0, p, 1)
        load_weight(nc, w2a_raw, w2a)
        load_x(1, 0, HOPS)
        load_weight(nc, w1a_raw, w1a)
        for i in range(2, TILES):
            load_x(i, 0, HOPS)

        identity = keep.tile([P, P], F32)
        make_identity(nc, identity[:])

        w2a_grouped = keep.tile([P, E, PACK], BF16, align_bytes=64)
        w1a_grouped = keep.tile([P, E, PACK], BF16, align_bytes=64)
        w2a_codes = keep.tile([P, E], U32, align_bytes=64)
        w1a_codes = keep.tile([P, E], U32, align_bytes=64)
        w2a_scales = keep.tile([P, E], U8, align_bytes=64)
        w1a_scales = keep.tile([P, E], U8, align_bytes=64)

        width = P * PACK
        turned = {}
        prepared = {}

        def turn(i, copy_out):
            x_words = x_rows[i][:].bitcast(F32)
            x_t = turns.tile([P, HOPS * width], BF16, align_bytes=64)
            x_t_words = x_t[:].bitcast(F32)
            banks = []
            for p in range(HOPS):
                bank = flipped.tile([P, 2, P], F32, name="bank")
                for u in range(2):
                    first = p * WORDS + u * P
                    nc.tensor.transpose(bank[:, u, :], x_words[:, first : first + P], identity[:])
                banks.append(bank)
            for p in range(HOPS):
                copy_out(
                    out=x_t_words[:, p * 2 * P : (p + 1) * 2 * P].rearrange(
                        "q (n u) -> q n u", u=2
                    ),
                    in_=banks[p][:].rearrange("q u n -> q n u"),
                )
            turned[i] = x_t

        def quantise_tile(i):
            x_t = turned[i]
            x_codes = operands.tile([P, HOPS * P], U32, align_bytes=64)
            x_scales = operands.tile([P, HOPS * P], U8, align_bytes=64)
            n_codes = operands.tile([P, HOPS * P], U32, align_bytes=64)
            n_scales = operands.tile([P, HOPS * P], U8, align_bytes=64)

            def quantise_x(p):
                nc.vector.quantize_mx(
                    out=x_codes[:, p * P : (p + 1) * P].bitcast(FP8X4),
                    scales=x_scales[:, p * P : (p + 1) * P],
                    in_=x_t[:, p * width : (p + 1) * width],
                )

            quantise_x(0)
            quantise_x(1)
            half = work.tile([P, HOPS, width], BF16)
            nc.vector.tensor_scalar(
                out=half[:].rearrange("q p w -> q (p w)"),
                in0=x_t[:],
                scalar1=0.5,
                scalar2=None,
                op0=MULT,
            )
            quantise_x(2)
            neigh = work.tile([P, HOPS, width], BF16, align_bytes=64)
            nc.vector.tensor_tensor(
                out=neigh[:, 0:2, :], in0=half[:, 0:2, :], in1=half[:, 1:3, :], op=ADD
            )
            nc.vector.tensor_tensor(
                out=neigh[:, 2, :], in0=half[:, 2, :], in1=half[:, 0, :], op=ADD
            )
            for s in range(HOPS):
                nc.vector.quantize_mx(
                    out=n_codes[:, s * P : (s + 1) * P].bitcast(FP8X4),
                    scales=n_scales[:, s * P : (s + 1) * P],
                    in_=neigh[:, s, :],
                )
            prepared[i] = (x_codes, x_scales, n_codes, n_scales)

        def multiply(i, p):
            x_codes, x_scales, n_codes, n_scales = prepared[i]
            items = slice(i * P, (i + 1) * P)
            own = slice(p * P, (p + 1) * P)
            slot = (p + 1) % HOPS
            others = slice(slot * P, (slot + 1) * P)
            result = results.tile([P, E], F32)
            for c in range(HALVES):
                cols = slice(c * N_PASS, (c + 1) * N_PASS)
                acc = sums.tile([P, N_PASS], F32)
                nc.tensor.matmul_mx(
                    out=acc[:],
                    lhsT=x_codes[:, own].bitcast(FP8X4),
                    lhsT_scale=x_scales[:, own],
                    rhs=w2a_codes[:, cols].bitcast(FP8X4),
                    rhs_scale=w2a_scales[:, cols],
                    start=True,
                    stop=False,
                )
                nc.tensor.matmul_mx(
                    out=acc[:],
                    lhsT=n_codes[:, others].bitcast(FP8X4),
                    lhsT_scale=n_scales[:, others],
                    rhs=w1a_codes[:, cols].bitcast(FP8X4),
                    rhs_scale=w1a_scales[:, cols],
                    start=False,
                    stop=True,
                )
                if i + AHEAD >= TILES and c == 1:
                    nc.vector.tensor_copy(out=result[:, cols], in_=acc[:])
                else:
                    nc.scalar.copy(out=result[:, cols], in_=acc[:])
                if i == TILES - 1:
                    nc.sync.dma_start(out=out[items, p, cols], in_=result[:, cols])
            if i < TILES - 1:
                nc.sync.dma_start(out=out[items, p, :], in_=result[:])

        turn(0, nc.scalar.copy)
        quantise_tile(0)
        for c in range(HALVES):
            regroup_weight(nc, w2a_raw, w2a_grouped, c)
        turn(1, nc.scalar.copy)
        for c in range(HALVES):
            quantise_weight(nc, w2a_grouped, w2a_codes, w2a_scales, c)
        for c in range(HALVES):
            regroup_weight(nc, w1a_raw, w1a_grouped, c)
        for c in range(HALVES):
            quantise_weight(nc, w1a_grouped, w1a_codes, w1a_scales, c)
        quantise_tile(1)
        turn(AHEAD, nc.vector.tensor_copy)

        for i in range(TILES):
            multiply(i, 0)
            if AHEAD < i + AHEAD < TILES:
                turn(i + AHEAD, nc.vector.tensor_copy)
            if i + AHEAD < TILES:
                quantise_tile(i + AHEAD)
            for p in range(1, HOPS):
                multiply(i, p)
